import numpy as np
import ml_dtypes


def mxq(x, axis, fmt="e4m3"):
    dtype, down = {"e4m3": (ml_dtypes.float8_e4m3fn, 7), "e5m2": (ml_dtypes.float8_e5m2, 14)}[fmt]
    v = np.moveaxis(np.asarray(x, np.float32).astype(ml_dtypes.bfloat16).astype(np.float64), axis, -1)
    blocks = v.reshape(v.shape[:-1] + (-1, 32))
    amax = np.abs(blocks).max(-1, keepdims=True)
    byte = np.maximum(np.where(amax > 0, np.frexp(amax)[1] - 1 + 127, 0) - down, 1)
    scale = np.exp2(byte - 127.0)
    codes = (blocks / scale).astype(np.float32).astype(dtype).astype(np.float64)
    return np.moveaxis((codes * scale).reshape(v.shape), -1, axis)


WIDE = False


def mx_kscale(k):
    if not WIDE:
        return np.ones(k)
    levels = np.array([10, -10, 5, -5, 0])
    a = np.random.permutation(np.resize(levels, k // 512 * 4)).reshape(k // 512, 4)
    idx = np.arange(k)
    return np.exp2(a[idx // 512, idx % 128 // 32])


BF16 = ml_dtypes.bfloat16


def bf(x):
    return np.asarray(x, np.float32).astype(BF16)


def f64(x):
    return np.asarray(x).astype(np.float64)


B, DIN, H1, H2, N, I, K, O = 1024, 2048, 1024, 512, 32, 16, 256, 16
NI = N * I
KO = K * O
SQ_EPS = 1e-8


def squash(t):
    sq = np.sum(t * t, axis=-1, keepdims=True)
    return (sq / (1.0 + sq)) * t / np.sqrt(sq + SQ_EPS)


def setup_inputs():
    s = mx_kscale(NI).reshape(N, I)
    return {"p": bf(np.random.standard_normal((B, N, I)) * s),
            "Wr": bf(np.random.standard_normal((N, K, O, I)) * K / np.sqrt(NI * O) / s[:, None, None, :])}


def reference(p, Wr):
    c = 1.0 / K
    pf = f64(p).reshape(B, NI)
    wf = f64(Wr).transpose(0, 3, 1, 2).reshape(NI, KO)
    s = (mxq(pf, 1, "e4m3") @ mxq(wf, 0, "e4m3")).reshape(B, K, O) * c
    return squash(s)

@@ -1,0 +1,286 @@
+from contextlib import ExitStack
+
+import concourse.mybir as mybir
+from concourse.masks import make_identity
+
+F32 = mybir.dt.float32
+BF16 = mybir.dt.bfloat16
+U32 = mybir.dt.uint32
+U8 = mybir.dt.uint8
+FP8X4 = mybir.dt.float8_e4m3fn_x4
+ACT = mybir.ActivationFunctionType
+ALU = mybir.AluOpType
+
+P = 128
+B = 1024
+K = 512
+I = 16
+J = 256
+O = 16
+COLS = J * O
+B_TILES = B // P
+N_HALF = 16
+BANK = 512
+J_BANK = BANK // O
+J_CHUNK = 64
+CHUNK = J_CHUNK * O
+N_CHUNKS = J // J_CHUNK
+TURNS_PER_BANK = BANK // P
+
+GROUP_BANKS = 4
+GROUP_J = GROUP_BANKS * J_BANK
+GROUPS_PER_CHUNK = B_TILES // 2
+N_GROUPS = N_CHUNKS * GROUPS_PER_CHUNK
+LAG_SUMS = 1
+LAG_FACTOR = 2
+LAG_OUTPUT = 3
+
+COUPLING = 1.0 / 256.0
+SQ_EPS = 1e-8
+SHRINK = 2.0 ** -32
+
+FLOPS = 2 * B * K * COLS
+
+
+def tile_capsulenetwork_pb_kernel(tc, p, Wr, out):
+    nc = tc.nc
+    out_rows = out.rearrange("(r t) j o -> r t (j o)", t=B_TILES)
+
+    with ExitStack() as ctx:
+        keep = ctx.enter_context(tc.tile_pool(name="keep", bufs=1))
+        wload = ctx.enter_context(tc.tile_pool(name="wload", bufs=N_CHUNKS))
+        stage = ctx.enter_context(tc.tile_pool(name="stage", bufs=2))
+        work = ctx.enter_context(tc.tile_pool(name="work", bufs=3))
+        results = ctx.enter_context(tc.tile_pool(name="results", bufs=4))
+        psum_turn = ctx.enter_context(tc.psum_pool(name="psum_turn", bufs=2))
+        psum_norm = ctx.enter_context(tc.psum_pool(name="psum_norm", bufs=3))
+        psum_out = ctx.enter_context(tc.psum_pool(name="psum_out", bufs=3))
+        ctx.enter_context(tc.manual_schedule())
+
+        def load_w_chunk(c):
+            w_raw = wload.tile([P, N_HALF, O * I], BF16)
+            for u in range(2):
+                nc.sync.dma_start(
+                    out=w_raw[u:P:2, :, :],
+                    in_=Wr[
+                        u * N_HALF : (u + 1) * N_HALF, c * J_CHUNK : (c + 1) * J_CHUNK, :, :
+                    ].rearrange("n j o i -> j n (o i)"),
+                )
+            return w_raw
+
+        w_raws = [load_w_chunk(0)]
+        p_raw = keep.tile([P, B_TILES * K], BF16)
+        nc.sync.dma_start(out=p_raw[:], in_=p.rearrange("(r t) n i -> r (t n i)", t=B_TILES))
+        w_raws.extend([load_w_chunk(c) for c in range(1, N_CHUNKS)])
+
+        shrink_col = keep.tile([P, 1], F32)
+        nc.vector.memset(shrink_col[:], SHRINK)
+        table_warmer = keep.tile([P, 1], F32)
+        nc.scalar.activation(out=table_warmer[:], in_=shrink_col[:], func=ACT.Abs_reciprocal_sqrt)
+
+        ident = keep.tile([P, P], F32)
+        make_identity(nc, ident[:])
+
+        p_codes = keep.tile([P, B_TILES * P], U32, align_bytes=64)
+        p_scales = keep.tile([P, B_TILES * P], U8, align_bytes=64)
+        w_codes = keep.tile([P, COLS], U32, align_bytes=64)
+        w_scales = keep.tile([P, COLS], U8, align_bytes=64)
+
+        def copy_out_of_psum(out_view, in_view, on_vector):
+            if on_vector:
+                nc.vector.tensor_copy(out=out_view, in_=in_view)
+            else:
+                nc.scalar.copy(out=out_view, in_=in_view)
+
+        w_sorted = {}
+        w_grouped = {}
+
+        def sort_w(c):
+            sorted_tile = stage.tile([P, O * N_HALF * I], BF16)
+            nc.vector.tensor_copy(
+                out=sorted_tile[:].rearrange("q (o n i) -> q o n i", o=O, i=I),
+                in_=w_raws[c][:].rearrange("q n (o i) -> q o n i", i=I),
+            )
+            w_sorted[c] = sorted_tile
+            grouped_tile = stage.tile([P, CHUNK * 4], BF16, align_bytes=64)
+            w_grouped[c] = grouped_tile
+
+        def turn_w(c, g, on_vector):
+            words = w_sorted[c][:].bitcast(F32)
+            turned = psum_turn.tile([P, TURNS_PER_BANK, P], F32)
+            for a in range(TURNS_PER_BANK):
+                o = TURNS_PER_BANK * g + a
+                nc.tensor.transpose(turned[:, a, :], words[:, o * P : (o + 1) * P], ident[:])
+            grouped_words = w_grouped[c][:].bitcast(F32).rearrange("m (j o u) -> m j o u", o=O, u=2)
+            copy_out_of_psum(
+                grouped_words[:, :, TURNS_PER_BANK * g : TURNS_PER_BANK * (g + 1), :],
+                turned[:].rearrange("m a (j u) -> m j a u", u=2),
+                on_vector,
+            )
+
+        def quantise_w(c):
+            chunk_cols = slice(c * CHUNK, (c + 1) * CHUNK)
+            nc.vector.quantize_mx(
+                out=w_codes[:, chunk_cols].bitcast(FP8X4),
+                scales=w_scales[:, chunk_cols],
+                in_=w_grouped[c][:],
+            )
+
+        sort_w(0)
+        for g in range(O // TURNS_PER_BANK):
+            turn_w(0, g, on_vector=(g % 2 == 1))
+        quantise_w(0)
+
+        p_words = p_raw[:].bitcast(F32)
+        p_grouped = keep.tile([P, B_TILES * P * 4], BF16, align_bytes=64)
+        p_grouped_words = p_grouped[:].bitcast(F32)
+        for pair in range(B_TILES // 2):
+            turned = psum_turn.tile([P, TURNS_PER_BANK, P], F32)
+            for tu in range(TURNS_PER_BANK):
+                first_word = (pair * TURNS_PER_BANK + tu) * P
+                nc.tensor.transpose(turned[:, tu, :], p_words[:, first_word : first_word + P], ident[:])
+            copy_out_of_psum(
+                p_grouped_words[:, pair * BANK : (pair + 1) * BANK].rearrange(
+                    "m (t r u) -> m t r u", t=2, u=2
+                ),
+                turned[:].rearrange("m (t u) r -> m t r u", u=2),
+                on_vector=(pair % 2 == 1),
+            )
+        nc.vector.quantize_mx(out=p_codes[:].bitcast(FP8X4), scales=p_scales[:], in_=p_grouped[:])
+
+        def product(acc, group, k):
+            t = 2 * (group % GROUPS_PER_CHUNK) + k // 2
+            first_col = (group // GROUPS_PER_CHUNK) * CHUNK + (k % 2) * BANK
+            nc.tensor.matmul_mx(
+                out=acc[:].rearrange("r j o -> r (j o)"),
+                lhsT=p_codes[:, t * P : (t + 1) * P].bitcast(FP8X4),
+                lhsT_scale=p_scales[:, t * P : (t + 1) * P],
+                rhs=w_codes[:, first_col : first_col + BANK].bitcast(FP8X4),
+                rhs_scale=w_scales[:, first_col : first_col + BANK],
+                start=True,
+                stop=True,
+            )
+
+        squares = {}
+        fours = {}
+        lengths = {}
+        denom_sq = {}
+        seeds = {}
+        factors = {}
+        result = {}
+
+        def square_bank(group, k):
+            if k == 0:
+                squares_tile = work.tile([P, GROUP_J, O], F32)
+                squares[group] = squares_tile
+            acc = psum_norm.tile([P, J_BANK, O], F32)
+            product(acc, group, k)
+            nc.scalar.activation(
+                out=squares[group][:, k * J_BANK : (k + 1) * J_BANK, :],
+                in_=acc[:],
+                func=ACT.Square,
+                scale=COUPLING,
+            )
+
+        def pair_sums(group):
+            eights = work.tile([P, GROUP_J, 8], F32)
+            nc.gpsimd.tensor_tensor(
+                out=eights[:], in0=squares[group][:, :, 0:8], in1=squares[group][:, :, 8:16], op=ALU.add
+            )
+            fours_tile = work.tile([P, GROUP_J, 4], F32)
+            nc.gpsimd.tensor_tensor(
+                out=fours_tile[:], in0=eights[:, :, 0:4], in1=eights[:, :, 4:8], op=ALU.add
+            )
+            fours[group] = fours_tile
+
+        def factor_step_lengths(group):
+            q = work.tile([P, GROUP_J], F32)
+            nc.vector.tensor_reduce(out=q[:], in_=fours[group][:], axis=mybir.AxisListType.X, op=ALU.add)
+            lengths[group] = q
+            one_plus_q_sq = work.tile([P, GROUP_J], F32)
+            nc.scalar.activation(
+                out=one_plus_q_sq[:], in_=q[:], func=ACT.Square, scale=SHRINK, bias=shrink_col[:]
+            )
+            denom_sq[group] = one_plus_q_sq
+
+        def factor_step_seed(group):
+            x = work.tile([P, GROUP_J], F32)
+            nc.vector.scalar_tensor_tensor(
+                out=x[:],
+                in0=lengths[group][:],
+                scalar=SQ_EPS,
+                in1=denom_sq[group][:],
+                op0=ALU.add,
+                op1=ALU.mult,
+            )
+            denom_sq[group] = x
+            y = work.tile([P, GROUP_J], F32)
+            nc.scalar.activation(out=y[:], in_=x[:], func=ACT.Abs_reciprocal_sqrt)
+            y_sq = work.tile([P, GROUP_J], F32)
+            nc.scalar.activation(out=y_sq[:], in_=y[:], func=ACT.Square)
+            seeds[group] = (y, y_sq)
+
+        def factor_step_newton(group):
+            y, y_sq = seeds[group]
+            x_y_sq = work.tile([P, GROUP_J], F32)
+            nc.vector.tensor_tensor(out=x_y_sq[:], in0=denom_sq[group][:], in1=y_sq[:], op=ALU.mult)
+            rough = work.tile([P, GROUP_J], F32)
+            nc.vector.scalar_tensor_tensor(
+                out=rough[:],
+                in0=lengths[group][:],
+                scalar=-0.5 * SHRINK * COUPLING,
+                in1=y[:],
+                op0=ALU.mult,
+                op1=ALU.mult,
+            )
+            factor = work.tile([P, GROUP_J], F32)
+            nc.vector.scalar_tensor_tensor(
+                out=factor[:], in0=x_y_sq[:], scalar=3.0, in1=rough[:], op0=ALU.subtract, op1=ALU.mult
+            )
+            factors[group] = factor
+
+        def output_bank(group, k):
+            acc = psum_out.tile([P, J_BANK, O], F32)
+            product(acc, group, k)
+            half = k % 2
+            if half == 0:
+                result_tile = results.tile([P, J_CHUNK, O], F32)
+                result[group] = result_tile
+            nc.vector.tensor_tensor(
+                out=result[group][:, half * J_BANK : (half + 1) * J_BANK, :],
+                in0=acc[:],
+                in1=factors[group][:, k * J_BANK : (k + 1) * J_BANK].unsqueeze(2).to_broadcast([P, J_BANK, O]),
+                op=ALU.mult,
+            )
+            if half == 1:
+                t = 2 * (group % GROUPS_PER_CHUNK) + k // 2
+                c = group // GROUPS_PER_CHUNK
+                nc.sync.dma_start(
+                    out=out_rows[:, t, c * CHUNK : (c + 1) * CHUNK],
+                    in_=result[group][:].rearrange("r j o -> r (j o)"),
+                )
+
+        for i in range(N_GROUPS + LAG_OUTPUT):
+            next_chunk = i // GROUPS_PER_CHUNK + 1
+            round_in_chunk = i % GROUPS_PER_CHUNK
+            prepare = next_chunk < N_CHUNKS
+            if prepare and round_in_chunk == 1:
+                sort_w(next_chunk)
+            if prepare and round_in_chunk == 3:
+                quantise_w(next_chunk)
+            if 0 <= i - LAG_SUMS < N_GROUPS:
+                pair_sums(i - LAG_SUMS)
+            for k in range(GROUP_BANKS):
+                if prepare and round_in_chunk == 2:
+                    turn_w(next_chunk, k, on_vector=False)
+                if i < N_GROUPS:
+                    square_bank(i, k)
+                if 0 <= i - LAG_FACTOR < N_GROUPS:
+                    if k == 0:
+                        factor_step_lengths(i - LAG_FACTOR)
+                    if k == 1:
+                        factor_step_seed(i - LAG_FACTOR)
+                    if k == 2:
+                        factor_step_newton(i - LAG_FACTOR)
+                if i >= LAG_OUTPUT:
+                    output_bank(i - LAG_OUTPUT, k)

@@ -51,7 +51,7 @@ def tile_capsulenetwork_pb_kernel(tc, p, Wr, out):
         wload = ctx.enter_context(tc.tile_pool(name="wload", bufs=N_CHUNKS))
         stage = ctx.enter_context(tc.tile_pool(name="stage", bufs=2))
         work = ctx.enter_context(tc.tile_pool(name="work", bufs=3))
-        results = ctx.enter_context(tc.tile_pool(name="results", bufs=4))
+        results = ctx.enter_context(tc.tile_pool(name="results", bufs=6))
         psum_turn = ctx.enter_context(tc.psum_pool(name="psum_turn", bufs=2))
         psum_norm = ctx.enter_context(tc.psum_pool(name="psum_norm", bufs=3))
         psum_out = ctx.enter_context(tc.psum_pool(name="psum_out", bufs=3))
@@ -134,6 +134,14 @@ def tile_capsulenetwork_pb_kernel(tc, p, Wr, out):
         p_words = p_raw[:].bitcast(F32)
         p_grouped = keep.tile([P, B_TILES * P * 4], BF16, align_bytes=64)
         p_grouped_words = p_grouped[:].bitcast(F32)
+
+        def quantise_p(pair):
+            nc.vector.quantize_mx(
+                out=p_codes[:, pair * 2 * P : (pair + 1) * 2 * P].bitcast(FP8X4),
+                scales=p_scales[:, pair * 2 * P : (pair + 1) * 2 * P],
+                in_=p_grouped[:, pair * 2 * P * 4 : (pair + 1) * 2 * P * 4],
+            )
+
         for pair in range(B_TILES // 2):
             turned = psum_turn.tile([P, TURNS_PER_BANK, P], F32)
             for tu in range(TURNS_PER_BANK):
@@ -146,7 +154,9 @@ def tile_capsulenetwork_pb_kernel(tc, p, Wr, out):
                 turned[:].rearrange("m (t u) r -> m t r u", u=2),
                 on_vector=(pair % 2 == 1),
             )
-        nc.vector.quantize_mx(out=p_codes[:].bitcast(FP8X4), scales=p_scales[:], in_=p_grouped[:])
+            if pair >= 1:
+                quantise_p(pair - 1)
+        quantise_p(B_TILES // 2 - 1)
 
         def product(acc, group, k):
             t = 2 * (group % GROUPS_PER_CHUNK) + k // 2
@@ -164,10 +174,10 @@ def tile_capsulenetwork_pb_kernel(tc, p, Wr, out):
         squares = {}
         fours = {}
         lengths = {}
+        one_plus_sq = {}
         denom_sq = {}
         seeds = {}
         factors = {}
-        result = {}
 
         def square_bank(group, k):
             if k == 0:
@@ -193,34 +203,38 @@ def tile_capsulenetwork_pb_kernel(tc, p, Wr, out):
             )
             fours[group] = fours_tile
 
-        def factor_step_lengths(group):
+        def factor_lengths(group):
             q = work.tile([P, GROUP_J], F32)
             nc.vector.tensor_reduce(out=q[:], in_=fours[group][:], axis=mybir.AxisListType.X, op=ALU.add)
             lengths[group] = q
+
+        def factor_one_plus_q(group):
             one_plus_q_sq = work.tile([P, GROUP_J], F32)
             nc.scalar.activation(
-                out=one_plus_q_sq[:], in_=q[:], func=ACT.Square, scale=SHRINK, bias=shrink_col[:]
+                out=one_plus_q_sq[:], in_=lengths[group][:], func=ACT.Square, scale=SHRINK, bias=shrink_col[:]
             )
-            denom_sq[group] = one_plus_q_sq
+            one_plus_sq[group] = one_plus_q_sq
 
-        def factor_step_seed(group):
+        def factor_denominator(group):
             x = work.tile([P, GROUP_J], F32)
             nc.vector.scalar_tensor_tensor(
                 out=x[:],
                 in0=lengths[group][:],
                 scalar=SQ_EPS,
-                in1=denom_sq[group][:],
+                in1=one_plus_sq[group][:],
                 op0=ALU.add,
                 op1=ALU.mult,
             )
             denom_sq[group] = x
+
+        def factor_seed(group):
             y = work.tile([P, GROUP_J], F32)
-            nc.scalar.activation(out=y[:], in_=x[:], func=ACT.Abs_reciprocal_sqrt)
+            nc.scalar.activation(out=y[:], in_=denom_sq[group][:], func=ACT.Abs_reciprocal_sqrt)
             y_sq = work.tile([P, GROUP_J], F32)
             nc.scalar.activation(out=y_sq[:], in_=y[:], func=ACT.Square)
             seeds[group] = (y, y_sq)
 
-        def factor_step_newton(group):
+        def factor_newton(group):
             y, y_sq = seeds[group]
             x_y_sq = work.tile([P, GROUP_J], F32)
             nc.vector.tensor_tensor(out=x_y_sq[:], in0=denom_sq[group][:], in1=y_sq[:], op=ALU.mult)
@@ -242,45 +256,42 @@ def tile_capsulenetwork_pb_kernel(tc, p, Wr, out):
         def output_bank(group, k):
             acc = psum_out.tile([P, J_BANK, O], F32)
             product(acc, group, k)
-            half = k % 2
-            if half == 0:
-                result_tile = results.tile([P, J_CHUNK, O], F32)
-                result[group] = result_tile
+            result = results.tile([P, J_BANK, O], F32)
             nc.vector.tensor_tensor(
-                out=result[group][:, half * J_BANK : (half + 1) * J_BANK, :],
+                out=result[:],
                 in0=acc[:],
                 in1=factors[group][:, k * J_BANK : (k + 1) * J_BANK].unsqueeze(2).to_broadcast([P, J_BANK, O]),
                 op=ALU.mult,
             )
-            if half == 1:
-                t = 2 * (group % GROUPS_PER_CHUNK) + k // 2
-                c = group // GROUPS_PER_CHUNK
-                nc.sync.dma_start(
-                    out=out_rows[:, t, c * CHUNK : (c + 1) * CHUNK],
-                    in_=result[group][:].rearrange("r j o -> r (j o)"),
-                )
+            t = 2 * (group % GROUPS_PER_CHUNK) + k // 2
+            first_col = (group // GROUPS_PER_CHUNK) * CHUNK + (k % 2) * BANK
+            nc.sync.dma_start(
+                out=out_rows[:, t, first_col : first_col + BANK], in_=result[:].rearrange("r j o -> r (j o)")
+            )
 
         for i in range(N_GROUPS + LAG_OUTPUT):
-            next_chunk = i // GROUPS_PER_CHUNK + 1
-            round_in_chunk = i % GROUPS_PER_CHUNK
-            prepare = next_chunk < N_CHUNKS
-            if prepare and round_in_chunk == 1:
-                sort_w(next_chunk)
-            if prepare and round_in_chunk == 3:
-                quantise_w(next_chunk)
+            prepare = 1 <= i < N_CHUNKS
+            if prepare:
+                sort_w(i)
             if 0 <= i - LAG_SUMS < N_GROUPS:
                 pair_sums(i - LAG_SUMS)
             for k in range(GROUP_BANKS):
-                if prepare and round_in_chunk == 2:
-                    turn_w(next_chunk, k, on_vector=False)
                 if i < N_GROUPS:
                     square_bank(i, k)
+                if k == 0 and i >= LAG_OUTPUT:
+                    factor_newton(i - LAG_OUTPUT)
                 if 0 <= i - LAG_FACTOR < N_GROUPS:
                     if k == 0:
-                        factor_step_lengths(i - LAG_FACTOR)
+                        factor_lengths(i - LAG_FACTOR)
                     if k == 1:
-                        factor_step_seed(i - LAG_FACTOR)
+                        factor_one_plus_q(i - LAG_FACTOR)
                     if k == 2:
-                        factor_step_newton(i - LAG_FACTOR)
+                        factor_denominator(i - LAG_FACTOR)
+                    if k == 3:
+                        factor_seed(i - LAG_FACTOR)
                 if i >= LAG_OUTPUT:
                     output_bank(i - LAG_OUTPUT, k)
+                if prepare:
+                    turn_w(i, k, on_vector=(i < LAG_OUTPUT))
+            if prepare:
+                quantise_w(i)

@@ -31,7 +31,6 @@ GROUP_BANKS = 4
 GROUP_J = GROUP_BANKS * J_BANK
 GROUPS_PER_CHUNK = B_TILES // 2
 N_GROUPS = N_CHUNKS * GROUPS_PER_CHUNK
-LAG_SUMS = 1
 LAG_FACTOR = 2
 LAG_OUTPUT = 3
 
@@ -172,7 +171,6 @@ def tile_capsulenetwork_pb_kernel(tc, p, Wr, out):
             )
 
         squares = {}
-        fours = {}
         lengths = {}
         one_plus_sq = {}
         denom_sq = {}
@@ -192,20 +190,9 @@ def tile_capsulenetwork_pb_kernel(tc, p, Wr, out):
                 scale=COUPLING,
             )
 
-        def pair_sums(group):
-            eights = work.tile([P, GROUP_J, 8], F32)
-            nc.gpsimd.tensor_tensor(
-                out=eights[:], in0=squares[group][:, :, 0:8], in1=squares[group][:, :, 8:16], op=ALU.add
-            )
-            fours_tile = work.tile([P, GROUP_J, 4], F32)
-            nc.gpsimd.tensor_tensor(
-                out=fours_tile[:], in0=eights[:, :, 0:4], in1=eights[:, :, 4:8], op=ALU.add
-            )
-            fours[group] = fours_tile
-
         def factor_lengths(group):
             q = work.tile([P, GROUP_J], F32)
-            nc.vector.tensor_reduce(out=q[:], in_=fours[group][:], axis=mybir.AxisListType.X, op=ALU.add)
+            nc.vector.tensor_reduce(out=q[:], in_=squares[group][:], axis=mybir.AxisListType.X, op=ALU.add)
             lengths[group] = q
 
         def factor_one_plus_q(group):
@@ -273,8 +260,6 @@ def tile_capsulenetwork_pb_kernel(tc, p, Wr, out):
             prepare = 1 <= i < N_CHUNKS
             if prepare:
                 sort_w(i)
-            if 0 <= i - LAG_SUMS < N_GROUPS:
-                pair_sums(i - LAG_SUMS)
             for k in range(GROUP_BANKS):
                 if i < N_GROUPS:
                     square_bank(i, k)

@@ -21,16 +21,19 @@ COLS = J * O
 B_TILES = B // P
 N_HALF = 16
 BANK = 512
-J_BANK = BANK // O
+QUARTERS = BANK // P
 J_CHUNK = 64
 CHUNK = J_CHUNK * O
 N_CHUNKS = J // J_CHUNK
-TURNS_PER_BANK = BANK // P
+O_PAIRS = CHUNK // P
+O_BANK = BANK // J_CHUNK
 
+GROUP_TILES = 2
 GROUP_BANKS = 4
-GROUP_J = GROUP_BANKS * J_BANK
-GROUPS_PER_CHUNK = B_TILES // 2
+GROUP_J = GROUP_TILES * J_CHUNK
+GROUPS_PER_CHUNK = B_TILES // GROUP_TILES
 N_GROUPS = N_CHUNKS * GROUPS_PER_CHUNK
+LAG_SUMS = 1
 LAG_FACTOR = 2
 LAG_OUTPUT = 3
 
@@ -50,9 +53,10 @@ def tile_capsulenetwork_pb_kernel(tc, p, Wr, out):
         wload = ctx.enter_context(tc.tile_pool(name="wload", bufs=N_CHUNKS))
         stage = ctx.enter_context(tc.tile_pool(name="stage", bufs=2))
         work = ctx.enter_context(tc.tile_pool(name="work", bufs=3))
-        results = ctx.enter_context(tc.tile_pool(name="results", bufs=6))
+        results = ctx.enter_context(tc.tile_pool(name="results", bufs=4))
         psum_turn = ctx.enter_context(tc.psum_pool(name="psum_turn", bufs=2))
-        psum_norm = ctx.enter_context(tc.psum_pool(name="psum_norm", bufs=3))
+        psum_norm = ctx.enter_context(tc.psum_pool(name="psum_norm", bufs=2))
+        psum_sums = ctx.enter_context(tc.psum_pool(name="psum_sums", bufs=1))
         psum_out = ctx.enter_context(tc.psum_pool(name="psum_out", bufs=3))
         ctx.enter_context(tc.manual_schedule())
 
@@ -106,15 +110,12 @@ def tile_capsulenetwork_pb_kernel(tc, p, Wr, out):
 
         def turn_w(c, g, on_vector):
             words = w_sorted[c][:].bitcast(F32)
-            turned = psum_turn.tile([P, TURNS_PER_BANK, P], F32)
-            for a in range(TURNS_PER_BANK):
-                o = TURNS_PER_BANK * g + a
-                nc.tensor.transpose(turned[:, a, :], words[:, o * P : (o + 1) * P], ident[:])
-            grouped_words = w_grouped[c][:].bitcast(F32).rearrange("m (j o u) -> m j o u", o=O, u=2)
+            turned = psum_turn.tile([P, BANK], F32)
+            for a in range(QUARTERS):
+                o = QUARTERS * g + a
+                nc.tensor.transpose(turned[:, a * P : (a + 1) * P], words[:, o * P : (o + 1) * P], ident[:])
             copy_out_of_psum(
-                grouped_words[:, :, TURNS_PER_BANK * g : TURNS_PER_BANK * (g + 1), :],
-                turned[:].rearrange("m a (j u) -> m j a u", u=2),
-                on_vector,
+                w_grouped[c][:].bitcast(F32)[:, g * BANK : (g + 1) * BANK], turned[:], on_vector
             )
 
         def quantise_w(c):
@@ -126,7 +127,7 @@ def tile_capsulenetwork_pb_kernel(tc, p, Wr, out):
             )
 
         sort_w(0)
-        for g in range(O // TURNS_PER_BANK):
+        for g in range(O // QUARTERS):
             turn_w(0, g, on_vector=(g % 2 == 1))
         quantise_w(0)
 
@@ -142,63 +143,92 @@ def tile_capsulenetwork_pb_kernel(tc, p, Wr, out):
             )
 
         for pair in range(B_TILES // 2):
-            turned = psum_turn.tile([P, TURNS_PER_BANK, P], F32)
-            for tu in range(TURNS_PER_BANK):
-                first_word = (pair * TURNS_PER_BANK + tu) * P
-                nc.tensor.transpose(turned[:, tu, :], p_words[:, first_word : first_word + P], ident[:])
+            turned = psum_turn.tile([P, BANK], F32)
+            for tu in range(QUARTERS):
+                first_word = (pair * QUARTERS + tu) * P
+                nc.tensor.transpose(
+                    turned[:, tu * P : (tu + 1) * P], p_words[:, first_word : first_word + P], ident[:]
+                )
             copy_out_of_psum(
                 p_grouped_words[:, pair * BANK : (pair + 1) * BANK].rearrange(
                     "m (t r u) -> m t r u", t=2, u=2
                 ),
-                turned[:].rearrange("m (t u) r -> m t r u", u=2),
+                turned[:].rearrange("m (t u r) -> m t r u", t=2, u=2),
                 on_vector=(pair % 2 == 1),
             )
             if pair >= 1:
                 quantise_p(pair - 1)
         quantise_p(B_TILES // 2 - 1)
 
-        def product(acc, group, k):
-            t = 2 * (group % GROUPS_PER_CHUNK) + k // 2
-            first_col = (group // GROUPS_PER_CHUNK) * CHUNK + (k % 2) * BANK
-            nc.tensor.matmul_mx(
-                out=acc[:].rearrange("r j o -> r (j o)"),
-                lhsT=p_codes[:, t * P : (t + 1) * P].bitcast(FP8X4),
-                lhsT_scale=p_scales[:, t * P : (t + 1) * P],
-                rhs=w_codes[:, first_col : first_col + BANK].bitcast(FP8X4),
-                rhs_scale=w_scales[:, first_col : first_col + BANK],
-                start=True,
-                stop=True,
-            )
+        def row_tile(group, k):
+            return GROUP_TILES * (group % GROUPS_PER_CHUNK) + k // 2
 
         squares = {}
+        pair_sums = {}
         lengths = {}
         one_plus_sq = {}
         denom_sq = {}
         seeds = {}
         factors = {}
+        result = {}
 
         def square_bank(group, k):
             if k == 0:
-                squares_tile = work.tile([P, GROUP_J, O], F32)
+                squares_tile = work.tile([P, GROUP_TILES, O_PAIRS, P], F32)
                 squares[group] = squares_tile
-            acc = psum_norm.tile([P, J_BANK, O], F32)
-            product(acc, group, k)
+            t = row_tile(group, k)
+            first_pair = (k % 2) * QUARTERS
+            acc = psum_norm.tile([P, QUARTERS, P], F32)
+            for a in range(QUARTERS):
+                first_col = (group // GROUPS_PER_CHUNK) * CHUNK + (first_pair + a) * P
+                nc.tensor.matmul_mx(
+                    out=acc[:, a, :],
+                    lhsT=w_codes[:, first_col : first_col + P].bitcast(FP8X4),
+                    lhsT_scale=w_scales[:, first_col : first_col + P],
+                    rhs=p_codes[:, t * P : (t + 1) * P].bitcast(FP8X4),
+                    rhs_scale=p_scales[:, t * P : (t + 1) * P],
+                    start=True,
+                    stop=True,
+                )
             nc.scalar.activation(
-                out=squares[group][:, k * J_BANK : (k + 1) * J_BANK, :],
+                out=squares[group][:, k // 2, first_pair : first_pair + QUARTERS, :],
                 in_=acc[:],
                 func=ACT.Square,
                 scale=COUPLING,
             )
 
+        def sum_squares(group):
+            sums = psum_sums.tile([P, GROUP_TILES, P], F32)
+            for tile_in_group in range(GROUP_TILES):
+                for pair in range(O_PAIRS):
+                    nc.tensor.matmul(
+                        out=sums[:, tile_in_group, :],
+                        lhsT=squares[group][:, tile_in_group, pair, :],
+                        rhs=ident[:],
+                        is_transpose=True,
+                        start=(pair == 0),
+                        stop=(pair == O_PAIRS - 1),
+                    )
+            pair_sums[group] = sums
+
         def factor_lengths(group):
-            q = work.tile([P, GROUP_J], F32)
-            nc.vector.tensor_reduce(out=q[:], in_=squares[group][:], axis=mybir.AxisListType.X, op=ALU.add)
+            q = work.tile([P, GROUP_TILES, J_CHUNK], F32)
+            nc.vector.tensor_reduce(
+                out=q[:],
+                in_=pair_sums[group][:].rearrange("r t (o j) -> r t j o", o=2),
+                axis=mybir.AxisListType.X,
+                op=ALU.add,
+            )
             lengths[group] = q
 
         def factor_one_plus_q(group):
             one_plus_q_sq = work.tile([P, GROUP_J], F32)
             nc.scalar.activation(
-                out=one_plus_q_sq[:], in_=lengths[group][:], func=ACT.Square, scale=SHRINK, bias=shrink_col[:]
+                out=one_plus_q_sq[:],
+                in_=lengths[group][:].rearrange("r t j -> r (t j)"),
+                func=ACT.Square,
+                scale=SHRINK,
+                bias=shrink_col[:],
             )
             one_plus_sq[group] = one_plus_q_sq
 
@@ -206,7 +236,7 @@ def tile_capsulenetwork_pb_kernel(tc, p, Wr, out):
             x = work.tile([P, GROUP_J], F32)
             nc.vector.scalar_tensor_tensor(
                 out=x[:],
-                in0=lengths[group][:],
+                in0=lengths[group][:].rearrange("r t j -> r (t j)"),
                 scalar=SQ_EPS,
                 in1=one_plus_sq[group][:],
                 op0=ALU.add,
@@ -228,7 +258,7 @@ def tile_capsulenetwork_pb_kernel(tc, p, Wr, out):
             rough = work.tile([P, GROUP_J], F32)
             nc.vector.scalar_tensor_tensor(
                 out=rough[:],
-                in0=lengths[group][:],
+                in0=lengths[group][:].rearrange("r t j -> r (t j)"),
                 scalar=-0.5 * SHRINK * COUPLING,
                 in1=y[:],
                 op0=ALU.mult,
@@ -241,20 +271,37 @@ def tile_capsulenetwork_pb_kernel(tc, p, Wr, out):
             factors[group] = factor
 
         def output_bank(group, k):
-            acc = psum_out.tile([P, J_BANK, O], F32)
-            product(acc, group, k)
-            result = results.tile([P, J_BANK, O], F32)
+            t = row_tile(group, k)
+            c = group // GROUPS_PER_CHUNK
+            half = k % 2
+            first_col = c * CHUNK + half * BANK
+            acc = psum_out.tile([P, O_BANK, J_CHUNK], F32)
+            nc.tensor.matmul_mx(
+                out=acc[:].rearrange("r o j -> r (o j)"),
+                lhsT=p_codes[:, t * P : (t + 1) * P].bitcast(FP8X4),
+                lhsT_scale=p_scales[:, t * P : (t + 1) * P],
+                rhs=w_codes[:, first_col : first_col + BANK].bitcast(FP8X4),
+                rhs_scale=w_scales[:, first_col : first_col + BANK],
+                start=True,
+                stop=True,
+            )
+            if half == 0:
+                result_tile = results.tile([P, J_CHUNK, O], F32)
+                result[group] = result_tile
+            tile_in_group = k // 2
             nc.vector.tensor_tensor(
-                out=result[:],
-                in0=acc[:],
-                in1=factors[group][:, k * J_BANK : (k + 1) * J_BANK].unsqueeze(2).to_broadcast([P, J_BANK, O]),
+                out=result[group][:, :, half * O_BANK : (half + 1) * O_BANK],
+                in0=acc[:].rearrange("r o j -> r j o"),
+                in1=factors[group][:, tile_in_group * J_CHUNK : (tile_in_group + 1) * J_CHUNK]
+                .unsqueeze(2)
+                .to_broadcast([P, J_CHUNK, O_BANK]),
                 op=ALU.mult,
             )
-            t = 2 * (group % GROUPS_PER_CHUNK) + k // 2
-            first_col = (group // GROUPS_PER_CHUNK) * CHUNK + (k % 2) * BANK
-            nc.sync.dma_start(
-                out=out_rows[:, t, first_col : first_col + BANK], in_=result[:].rearrange("r j o -> r (j o)")
-            )
+            if half == 1:
+                nc.sync.dma_start(
+                    out=out_rows[:, t, c * CHUNK : (c + 1) * CHUNK],
+                    in_=result[group][:].rearrange("r j o -> r (j o)"),
+                )
 
         for i in range(N_GROUPS + LAG_OUTPUT):
             prepare = 1 <= i < N_CHUNKS
@@ -280,3 +327,5 @@ def tile_capsulenetwork_pb_kernel(tc, p, Wr, out):
                     turn_w(i, k, on_vector=(i < LAG_OUTPUT))
             if prepare:
                 quantise_w(i)
+            if 0 <= i - LAG_SUMS < N_GROUPS:
+                sum_squares(i - LAG_SUMS)

@@ -25,8 +25,11 @@ QUARTERS = BANK // P
 J_CHUNK = 64
 CHUNK = J_CHUNK * O
 N_CHUNKS = J // J_CHUNK
-O_PAIRS = CHUNK // P
-O_BANK = BANK // J_CHUNK
+O_LOW = 4
+O_HIGH = O // O_LOW
+J_BLOCK = P // O_LOW
+BLOCKS_PER_HIGH = J_CHUNK // J_BLOCK
+HIGH_PER_BANK = BANK // (J_CHUNK * O_LOW)
 
 GROUP_TILES = 2
 GROUP_BANKS = 4
@@ -111,11 +114,15 @@ def tile_capsulenetwork_pb_kernel(tc, p, Wr, out):
         def turn_w(c, g, on_vector):
             words = w_sorted[c][:].bitcast(F32)
             turned = psum_turn.tile([P, BANK], F32)
-            for a in range(QUARTERS):
-                o = QUARTERS * g + a
-                nc.tensor.transpose(turned[:, a * P : (a + 1) * P], words[:, o * P : (o + 1) * P], ident[:])
+            for ol in range(O_LOW):
+                o = O_LOW * g + ol
+                nc.tensor.transpose(turned[:, ol * P : (ol + 1) * P], words[:, o * P : (o + 1) * P], ident[:])
             copy_out_of_psum(
-                w_grouped[c][:].bitcast(F32)[:, g * BANK : (g + 1) * BANK], turned[:], on_vector
+                w_grouped[c][:].bitcast(F32)[:, g * BANK : (g + 1) * BANK].rearrange(
+                    "m (j l u) -> m j l u", l=O_LOW, u=2
+                ),
+                turned[:].rearrange("m (l j u) -> m j l u", l=O_LOW, u=2),
+                on_vector,
             )
 
         def quantise_w(c):
@@ -127,7 +134,7 @@ def tile_capsulenetwork_pb_kernel(tc, p, Wr, out):
             )
 
         sort_w(0)
-        for g in range(O // QUARTERS):
+        for g in range(O_HIGH):
             turn_w(0, g, on_vector=(g % 2 == 1))
         quantise_w(0)
 
@@ -160,11 +167,8 @@ def tile_capsulenetwork_pb_kernel(tc, p, Wr, out):
                 quantise_p(pair - 1)
         quantise_p(B_TILES // 2 - 1)
 
-        def row_tile(group, k):
-            return GROUP_TILES * (group % GROUPS_PER_CHUNK) + k // 2
-
         squares = {}
-        pair_sums = {}
+        partial_sums = {}
         lengths = {}
         one_plus_sq = {}
         denom_sq = {}
@@ -172,50 +176,52 @@ def tile_capsulenetwork_pb_kernel(tc, p, Wr, out):
         factors = {}
         result = {}
 
-        def square_bank(group, k):
-            if k == 0:
-                squares_tile = work.tile([P, GROUP_TILES, O_PAIRS, P], F32)
+        def square_bank(group, oh):
+            if oh == 0:
+                squares_tile = work.tile([P, O_HIGH * BLOCKS_PER_HIGH, GROUP_TILES, P], F32)
                 squares[group] = squares_tile
-            t = row_tile(group, k)
-            first_pair = (k % 2) * QUARTERS
-            acc = psum_norm.tile([P, QUARTERS, P], F32)
-            for a in range(QUARTERS):
-                first_col = (group // GROUPS_PER_CHUNK) * CHUNK + (first_pair + a) * P
+            first_row = (group % GROUPS_PER_CHUNK) * GROUP_TILES * P
+            acc = psum_norm.tile([P, BLOCKS_PER_HIGH, GROUP_TILES * P], F32)
+            for block in range(BLOCKS_PER_HIGH):
+                first_col = (group // GROUPS_PER_CHUNK) * CHUNK + (oh * BLOCKS_PER_HIGH + block) * P
                 nc.tensor.matmul_mx(
-                    out=acc[:, a, :],
+                    out=acc[:, block, :],
                     lhsT=w_codes[:, first_col : first_col + P].bitcast(FP8X4),
                     lhsT_scale=w_scales[:, first_col : first_col + P],
-                    rhs=p_codes[:, t * P : (t + 1) * P].bitcast(FP8X4),
-                    rhs_scale=p_scales[:, t * P : (t + 1) * P],
+                    rhs=p_codes[:, first_row : first_row + GROUP_TILES * P].bitcast(FP8X4),
+                    rhs_scale=p_scales[:, first_row : first_row + GROUP_TILES * P],
                     start=True,
                     stop=True,
                 )
             nc.scalar.activation(
-                out=squares[group][:, k // 2, first_pair : first_pair + QUARTERS, :],
+                out=squares[group][:, oh * BLOCKS_PER_HIGH : (oh + 1) * BLOCKS_PER_HIGH, :, :].rearrange(
+                    "q b t r -> q b (t r)"
+                ),
                 in_=acc[:],
                 func=ACT.Square,
                 scale=COUPLING,
             )
 
         def sum_squares(group):
-            sums = psum_sums.tile([P, GROUP_TILES, P], F32)
+            sums = psum_sums.tile([P, GROUP_TILES, BLOCKS_PER_HIGH, P], F32)
             for tile_in_group in range(GROUP_TILES):
-                for pair in range(O_PAIRS):
-                    nc.tensor.matmul(
-                        out=sums[:, tile_in_group, :],
-                        lhsT=squares[group][:, tile_in_group, pair, :],
-                        rhs=ident[:],
-                        is_transpose=True,
-                        start=(pair == 0),
-                        stop=(pair == O_PAIRS - 1),
-                    )
-            pair_sums[group] = sums
+                for block in range(BLOCKS_PER_HIGH):
+                    for oh in range(O_HIGH):
+                        nc.tensor.matmul(
+                            out=sums[:, tile_in_group, block, :],
+                            lhsT=squares[group][:, oh * BLOCKS_PER_HIGH + block, tile_in_group, :],
+                            rhs=ident[:],
+                            is_transpose=True,
+                            start=(oh == 0),
+                            stop=(oh == O_HIGH - 1),
+                        )
+            partial_sums[group] = sums
 
         def factor_lengths(group):
-            q = work.tile([P, GROUP_TILES, J_CHUNK], F32)
+            q = work.tile([P, GROUP_J], F32)
             nc.vector.tensor_reduce(
                 out=q[:],
-                in_=pair_sums[group][:].rearrange("r t (o j) -> r t j o", o=2),
+                in_=partial_sums[group][:].rearrange("r t b (j l) -> r (t b j) l", l=O_LOW),
                 axis=mybir.AxisListType.X,
                 op=ALU.add,
             )
@@ -225,7 +231,7 @@ def tile_capsulenetwork_pb_kernel(tc, p, Wr, out):
             one_plus_q_sq = work.tile([P, GROUP_J], F32)
             nc.scalar.activation(
                 out=one_plus_q_sq[:],
-                in_=lengths[group][:].rearrange("r t j -> r (t j)"),
+                in_=lengths[group][:],
                 func=ACT.Square,
                 scale=SHRINK,
                 bias=shrink_col[:],
@@ -236,7 +242,7 @@ def tile_capsulenetwork_pb_kernel(tc, p, Wr, out):
             x = work.tile([P, GROUP_J], F32)
             nc.vector.scalar_tensor_tensor(
                 out=x[:],
-                in0=lengths[group][:].rearrange("r t j -> r (t j)"),
+                in0=lengths[group][:],
                 scalar=SQ_EPS,
                 in1=one_plus_sq[group][:],
                 op0=ALU.add,
@@ -258,7 +264,7 @@ def tile_capsulenetwork_pb_kernel(tc, p, Wr, out):
             rough = work.tile([P, GROUP_J], F32)
             nc.vector.scalar_tensor_tensor(
                 out=rough[:],
-                in0=lengths[group][:].rearrange("r t j -> r (t j)"),
+                in0=lengths[group][:],
                 scalar=-0.5 * SHRINK * COUPLING,
                 in1=y[:],
                 op0=ALU.mult,
@@ -271,13 +277,14 @@ def tile_capsulenetwork_pb_kernel(tc, p, Wr, out):
             factors[group] = factor
 
         def output_bank(group, k):
-            t = row_tile(group, k)
-            c = group // GROUPS_PER_CHUNK
+            tile_in_group = k // 2
             half = k % 2
+            t = GROUP_TILES * (group % GROUPS_PER_CHUNK) + tile_in_group
+            c = group // GROUPS_PER_CHUNK
             first_col = c * CHUNK + half * BANK
-            acc = psum_out.tile([P, O_BANK, J_CHUNK], F32)
+            acc = psum_out.tile([P, HIGH_PER_BANK, J_CHUNK, O_LOW], F32)
             nc.tensor.matmul_mx(
-                out=acc[:].rearrange("r o j -> r (o j)"),
+                out=acc[:].rearrange("r h j l -> r (h j l)"),
                 lhsT=p_codes[:, t * P : (t + 1) * P].bitcast(FP8X4),
                 lhsT_scale=p_scales[:, t * P : (t + 1) * P],
                 rhs=w_codes[:, first_col : first_col + BANK].bitcast(FP8X4),
@@ -286,21 +293,21 @@ def tile_capsulenetwork_pb_kernel(tc, p, Wr, out):
                 stop=True,
             )
             if half == 0:
-                result_tile = results.tile([P, J_CHUNK, O], F32)
+                result_tile = results.tile([P, J_CHUNK, O_HIGH, O_LOW], F32)
                 result[group] = result_tile
-            tile_in_group = k // 2
             nc.vector.tensor_tensor(
-                out=result[group][:, :, half * O_BANK : (half + 1) * O_BANK],
-                in0=acc[:].rearrange("r o j -> r j o"),
+                out=result[group][:, :, half * HIGH_PER_BANK : (half + 1) * HIGH_PER_BANK, :],
+                in0=acc[:].rearrange("r h j l -> r j h l"),
                 in1=factors[group][:, tile_in_group * J_CHUNK : (tile_in_group + 1) * J_CHUNK]
                 .unsqueeze(2)
-                .to_broadcast([P, J_CHUNK, O_BANK]),
+                .unsqueeze(3)
+                .to_broadcast([P, J_CHUNK, HIGH_PER_BANK, O_LOW]),
                 op=ALU.mult,
             )
             if half == 1:
                 nc.sync.dma_start(
                     out=out_rows[:, t, c * CHUNK : (c + 1) * CHUNK],
-                    in_=result[group][:].rearrange("r j o -> r (j o)"),
+                    in_=result[group][:].rearrange("r j h l -> r (j h l)"),
                 )
 
         for i in range(N_GROUPS + LAG_OUTPUT):

@@ -61,7 +61,6 @@ def tile_capsulenetwork_pb_kernel(tc, p, Wr, out):
         psum_norm = ctx.enter_context(tc.psum_pool(name="psum_norm", bufs=2))
         psum_sums = ctx.enter_context(tc.psum_pool(name="psum_sums", bufs=1))
         psum_out = ctx.enter_context(tc.psum_pool(name="psum_out", bufs=3))
-        ctx.enter_context(tc.manual_schedule())
 
         def load_w_chunk(c):
             w_raw = wload.tile([P, N_HALF, O * I], BF16)

@@ -12,6 +12,8 @@ ACT = mybir.ActivationFunctionType
 ALU = mybir.AluOpType
 
 P = 128
+PACK = 4
+HALVES = 2
 B = 1024
 K = 512
 I = 16
@@ -19,23 +21,22 @@ J = 256
 O = 16
 COLS = J * O
 B_TILES = B // P
-N_HALF = 16
+N_HALF = K // I // HALVES
 BANK = 512
 QUARTERS = BANK // P
 J_CHUNK = 64
 CHUNK = J_CHUNK * O
 N_CHUNKS = J // J_CHUNK
-O_LOW = 4
-O_HIGH = O // O_LOW
-J_BLOCK = P // O_LOW
-BLOCKS_PER_HIGH = J_CHUNK // J_BLOCK
-HIGH_PER_BANK = BANK // (J_CHUNK * O_LOW)
+O_PER_OPERAND = P // J_CHUNK
+O_PAIRS = O // O_PER_OPERAND
+O_PER_BANK = BANK // J_CHUNK
 
 GROUP_TILES = 2
-GROUP_BANKS = 4
+GROUP_ROWS = GROUP_TILES * P
 GROUP_J = GROUP_TILES * J_CHUNK
 GROUPS_PER_CHUNK = B_TILES // GROUP_TILES
 N_GROUPS = N_CHUNKS * GROUPS_PER_CHUNK
+OPERANDS_PER_BANK = BANK // GROUP_ROWS
 LAG_SUMS = 1
 LAG_FACTOR = 2
 LAG_OUTPUT = 3
@@ -54,19 +55,18 @@ def tile_capsulenetwork_pb_kernel(tc, p, Wr, out):
     with ExitStack() as ctx:
         keep = ctx.enter_context(tc.tile_pool(name="keep", bufs=1))
         wload = ctx.enter_context(tc.tile_pool(name="wload", bufs=N_CHUNKS))
-        stage = ctx.enter_context(tc.tile_pool(name="stage", bufs=2))
+        wprep = ctx.enter_context(tc.tile_pool(name="wprep", bufs=2))
         work = ctx.enter_context(tc.tile_pool(name="work", bufs=3))
-        results = ctx.enter_context(tc.tile_pool(name="results", bufs=4))
-        psum_turn = ctx.enter_context(tc.psum_pool(name="psum_turn", bufs=2))
-        psum_norm = ctx.enter_context(tc.psum_pool(name="psum_norm", bufs=2))
-        psum_sums = ctx.enter_context(tc.psum_pool(name="psum_sums", bufs=1))
+        results = ctx.enter_context(tc.tile_pool(name="results", bufs=2 * GROUP_TILES))
+        psum_brief = ctx.enter_context(tc.psum_pool(name="psum_brief", bufs=3))
+        psum_sums = ctx.enter_context(tc.psum_pool(name="psum_sums", bufs=2))
         psum_out = ctx.enter_context(tc.psum_pool(name="psum_out", bufs=3))
 
         def load_w_chunk(c):
             w_raw = wload.tile([P, N_HALF, O * I], BF16)
-            for u in range(2):
+            for u in range(HALVES):
                 nc.sync.dma_start(
-                    out=w_raw[u:P:2, :, :],
+                    out=w_raw[u:P:HALVES, :, :],
                     in_=Wr[
                         u * N_HALF : (u + 1) * N_HALF, c * J_CHUNK : (c + 1) * J_CHUNK, :, :
                     ].rearrange("n j o i -> j n (o i)"),
@@ -91,183 +91,128 @@ def tile_capsulenetwork_pb_kernel(tc, p, Wr, out):
         w_codes = keep.tile([P, COLS], U32, align_bytes=64)
         w_scales = keep.tile([P, COLS], U8, align_bytes=64)
 
-        def copy_out_of_psum(out_view, in_view, on_vector):
-            if on_vector:
-                nc.vector.tensor_copy(out=out_view, in_=in_view)
-            else:
+        def copy_out_of_psum(bank, out_view, in_view):
+            if bank % 2 == 0:
                 nc.scalar.copy(out=out_view, in_=in_view)
+            else:
+                nc.vector.tensor_copy(out=out_view, in_=in_view)
 
-        w_sorted = {}
-        w_grouped = {}
-
-        def sort_w(c):
-            sorted_tile = stage.tile([P, O * N_HALF * I], BF16)
+        def prepare_w(c):
+            w_sorted = wprep.tile([P, O * N_HALF * I], BF16)
             nc.vector.tensor_copy(
-                out=sorted_tile[:].rearrange("q (o n i) -> q o n i", o=O, i=I),
+                out=w_sorted[:].rearrange("q (o n i) -> q o n i", o=O, i=I),
                 in_=w_raws[c][:].rearrange("q n (o i) -> q o n i", i=I),
             )
-            w_sorted[c] = sorted_tile
-            grouped_tile = stage.tile([P, CHUNK * 4], BF16, align_bytes=64)
-            w_grouped[c] = grouped_tile
-
-        def turn_w(c, g, on_vector):
-            words = w_sorted[c][:].bitcast(F32)
-            turned = psum_turn.tile([P, BANK], F32)
-            for ol in range(O_LOW):
-                o = O_LOW * g + ol
-                nc.tensor.transpose(turned[:, ol * P : (ol + 1) * P], words[:, o * P : (o + 1) * P], ident[:])
-            copy_out_of_psum(
-                w_grouped[c][:].bitcast(F32)[:, g * BANK : (g + 1) * BANK].rearrange(
-                    "m (j l u) -> m j l u", l=O_LOW, u=2
-                ),
-                turned[:].rearrange("m (l j u) -> m j l u", l=O_LOW, u=2),
-                on_vector,
-            )
-
-        def quantise_w(c):
+            w_words = w_sorted[:].bitcast(F32)
+            w_grouped = wprep.tile([P, CHUNK * PACK], BF16, align_bytes=64)
+            for bank in range(O // QUARTERS):
+                turned = psum_brief.tile([P, BANK], F32, tag="brief")
+                for quarter in range(QUARTERS):
+                    o = QUARTERS * bank + quarter
+                    nc.tensor.transpose(
+                        turned[:, quarter * P : (quarter + 1) * P], w_words[:, o * P : (o + 1) * P], ident[:]
+                    )
+                copy_out_of_psum(bank, w_grouped[:].bitcast(F32)[:, bank * BANK : (bank + 1) * BANK], turned[:])
             chunk_cols = slice(c * CHUNK, (c + 1) * CHUNK)
             nc.vector.quantize_mx(
-                out=w_codes[:, chunk_cols].bitcast(FP8X4),
-                scales=w_scales[:, chunk_cols],
-                in_=w_grouped[c][:],
+                out=w_codes[:, chunk_cols].bitcast(FP8X4), scales=w_scales[:, chunk_cols], in_=w_grouped[:]
             )
 
-        sort_w(0)
-        for g in range(O_HIGH):
-            turn_w(0, g, on_vector=(g % 2 == 1))
-        quantise_w(0)
-
-        p_words = p_raw[:].bitcast(F32)
-        p_grouped = keep.tile([P, B_TILES * P * 4], BF16, align_bytes=64)
-        p_grouped_words = p_grouped[:].bitcast(F32)
-
-        def quantise_p(pair):
-            nc.vector.quantize_mx(
-                out=p_codes[:, pair * 2 * P : (pair + 1) * 2 * P].bitcast(FP8X4),
-                scales=p_scales[:, pair * 2 * P : (pair + 1) * 2 * P],
-                in_=p_grouped[:, pair * 2 * P * 4 : (pair + 1) * 2 * P * 4],
-            )
-
-        for pair in range(B_TILES // 2):
-            turned = psum_turn.tile([P, BANK], F32)
-            for tu in range(QUARTERS):
-                first_word = (pair * QUARTERS + tu) * P
-                nc.tensor.transpose(
-                    turned[:, tu * P : (tu + 1) * P], p_words[:, first_word : first_word + P], ident[:]
+        def prepare_p():
+            p_words = p_raw[:].bitcast(F32)
+            p_grouped = keep.tile([P, B_TILES * P * PACK], BF16, align_bytes=64)
+            p_grouped_words = p_grouped[:].bitcast(F32)
+            for bank in range(GROUPS_PER_CHUNK):
+                turned = psum_brief.tile([P, BANK], F32, tag="brief")
+                for quarter in range(QUARTERS):
+                    first_word = (bank * QUARTERS + quarter) * P
+                    nc.tensor.transpose(
+                        turned[:, quarter * P : (quarter + 1) * P],
+                        p_words[:, first_word : first_word + P],
+                        ident[:],
+                    )
+                copy_out_of_psum(
+                    bank,
+                    p_grouped_words[:, bank * BANK : (bank + 1) * BANK].rearrange(
+                        "m (t r u) -> m t r u", t=GROUP_TILES, u=HALVES
+                    ),
+                    turned[:].rearrange("m (t u r) -> m t r u", t=GROUP_TILES, u=HALVES),
                 )
-            copy_out_of_psum(
-                p_grouped_words[:, pair * BANK : (pair + 1) * BANK].rearrange(
-                    "m (t r u) -> m t r u", t=2, u=2
-                ),
-                turned[:].rearrange("m (t u r) -> m t r u", t=2, u=2),
-                on_vector=(pair % 2 == 1),
-            )
-            if pair >= 1:
-                quantise_p(pair - 1)
-        quantise_p(B_TILES // 2 - 1)
+            for bank in range(GROUPS_PER_CHUNK):
+                rows = slice(bank * GROUP_ROWS, (bank + 1) * GROUP_ROWS)
+                nc.vector.quantize_mx(
+                    out=p_codes[:, rows].bitcast(FP8X4),
+                    scales=p_scales[:, rows],
+                    in_=p_grouped[:, bank * GROUP_ROWS * PACK : (bank + 1) * GROUP_ROWS * PACK],
+                )
 
         squares = {}
-        partial_sums = {}
-        lengths = {}
-        one_plus_sq = {}
-        denom_sq = {}
-        seeds = {}
+        pair_sums = {}
         factors = {}
-        result = {}
 
-        def square_bank(group, oh):
-            if oh == 0:
-                squares_tile = work.tile([P, O_HIGH * BLOCKS_PER_HIGH, GROUP_TILES, P], F32)
-                squares[group] = squares_tile
-            first_row = (group % GROUPS_PER_CHUNK) * GROUP_TILES * P
-            acc = psum_norm.tile([P, BLOCKS_PER_HIGH, GROUP_TILES * P], F32)
-            for block in range(BLOCKS_PER_HIGH):
-                first_col = (group // GROUPS_PER_CHUNK) * CHUNK + (oh * BLOCKS_PER_HIGH + block) * P
-                nc.tensor.matmul_mx(
-                    out=acc[:, block, :],
-                    lhsT=w_codes[:, first_col : first_col + P].bitcast(FP8X4),
-                    lhsT_scale=w_scales[:, first_col : first_col + P],
-                    rhs=p_codes[:, first_row : first_row + GROUP_TILES * P].bitcast(FP8X4),
-                    rhs_scale=p_scales[:, first_row : first_row + GROUP_TILES * P],
-                    start=True,
-                    stop=True,
+        def stage_squares(group):
+            first_row = (group % GROUPS_PER_CHUNK) * GROUP_ROWS
+            squares_tile = work.tile([P, O_PAIRS, GROUP_ROWS], F32)
+            for bank in range(O_PAIRS // OPERANDS_PER_BANK):
+                acc = psum_brief.tile([P, OPERANDS_PER_BANK, GROUP_ROWS], F32, tag="brief")
+                for operand in range(OPERANDS_PER_BANK):
+                    first_col = (group // GROUPS_PER_CHUNK) * CHUNK + (bank * OPERANDS_PER_BANK + operand) * P
+                    nc.tensor.matmul_mx(
+                        out=acc[:, operand, :],
+                        lhsT=w_codes[:, first_col : first_col + P].bitcast(FP8X4),
+                        lhsT_scale=w_scales[:, first_col : first_col + P],
+                        rhs=p_codes[:, first_row : first_row + GROUP_ROWS].bitcast(FP8X4),
+                        rhs_scale=p_scales[:, first_row : first_row + GROUP_ROWS],
+                        start=True,
+                        stop=True,
+                    )
+                nc.scalar.activation(
+                    out=squares_tile[:, bank * OPERANDS_PER_BANK : (bank + 1) * OPERANDS_PER_BANK, :],
+                    in_=acc[:],
+                    func=ACT.Square,
+                    scale=COUPLING,
                 )
-            nc.scalar.activation(
-                out=squares[group][:, oh * BLOCKS_PER_HIGH : (oh + 1) * BLOCKS_PER_HIGH, :, :].rearrange(
-                    "q b t r -> q b (t r)"
-                ),
-                in_=acc[:],
-                func=ACT.Square,
-                scale=COUPLING,
-            )
+            squares[group] = squares_tile
 
-        def sum_squares(group):
-            sums = psum_sums.tile([P, GROUP_TILES, BLOCKS_PER_HIGH, P], F32)
+        def stage_sums(group):
+            sums = psum_sums.tile([P, GROUP_TILES, P], F32)
             for tile_in_group in range(GROUP_TILES):
-                for block in range(BLOCKS_PER_HIGH):
-                    for oh in range(O_HIGH):
-                        nc.tensor.matmul(
-                            out=sums[:, tile_in_group, block, :],
-                            lhsT=squares[group][:, oh * BLOCKS_PER_HIGH + block, tile_in_group, :],
-                            rhs=ident[:],
-                            is_transpose=True,
-                            start=(oh == 0),
-                            stop=(oh == O_HIGH - 1),
-                        )
-            partial_sums[group] = sums
+                for o_pair in range(O_PAIRS):
+                    nc.tensor.matmul(
+                        out=sums[:, tile_in_group, :],
+                        lhsT=squares[group][:, o_pair, tile_in_group * P : (tile_in_group + 1) * P],
+                        rhs=ident[:],
+                        is_transpose=True,
+                        start=(o_pair == 0),
+                        stop=(o_pair == O_PAIRS - 1),
+                    )
+            pair_sums[group] = sums
 
-        def factor_lengths(group):
+        def stage_factor(group):
             q = work.tile([P, GROUP_J], F32)
             nc.vector.tensor_reduce(
-                out=q[:],
-                in_=partial_sums[group][:].rearrange("r t b (j l) -> r (t b j) l", l=O_LOW),
+                out=q[:].rearrange("r (t j) -> r t j", t=GROUP_TILES),
+                in_=pair_sums[group][:].rearrange("r t (o j) -> r t j o", o=O_PER_OPERAND),
                 axis=mybir.AxisListType.X,
                 op=ALU.add,
             )
-            lengths[group] = q
-
-        def factor_one_plus_q(group):
             one_plus_q_sq = work.tile([P, GROUP_J], F32)
             nc.scalar.activation(
-                out=one_plus_q_sq[:],
-                in_=lengths[group][:],
-                func=ACT.Square,
-                scale=SHRINK,
-                bias=shrink_col[:],
+                out=one_plus_q_sq[:], in_=q[:], func=ACT.Square, scale=SHRINK, bias=shrink_col[:]
             )
-            one_plus_sq[group] = one_plus_q_sq
-
-        def factor_denominator(group):
             x = work.tile([P, GROUP_J], F32)
             nc.vector.scalar_tensor_tensor(
-                out=x[:],
-                in0=lengths[group][:],
-                scalar=SQ_EPS,
-                in1=one_plus_sq[group][:],
-                op0=ALU.add,
-                op1=ALU.mult,
+                out=x[:], in0=q[:], scalar=SQ_EPS, in1=one_plus_q_sq[:], op0=ALU.add, op1=ALU.mult
             )
-            denom_sq[group] = x
-
-        def factor_seed(group):
             y = work.tile([P, GROUP_J], F32)
-            nc.scalar.activation(out=y[:], in_=denom_sq[group][:], func=ACT.Abs_reciprocal_sqrt)
+            nc.scalar.activation(out=y[:], in_=x[:], func=ACT.Abs_reciprocal_sqrt)
             y_sq = work.tile([P, GROUP_J], F32)
             nc.scalar.activation(out=y_sq[:], in_=y[:], func=ACT.Square)
-            seeds[group] = (y, y_sq)
-
-        def factor_newton(group):
-            y, y_sq = seeds[group]
             x_y_sq = work.tile([P, GROUP_J], F32)
-            nc.vector.tensor_tensor(out=x_y_sq[:], in0=denom_sq[group][:], in1=y_sq[:], op=ALU.mult)
+            nc.vector.tensor_tensor(out=x_y_sq[:], in0=x[:], in1=y_sq[:], op=ALU.mult)
             rough = work.tile([P, GROUP_J], F32)
             nc.vector.scalar_tensor_tensor(
-                out=rough[:],
-                in0=lengths[group][:],
-                scalar=-0.5 * SHRINK * COUPLING,
-                in1=y[:],
-                op0=ALU.mult,
-                op1=ALU.mult,
+                out=rough[:], in0=q[:], scalar=-0.5 * SHRINK * COUPLING, in1=y[:], op0=ALU.mult, op1=ALU.mult
             )
             factor = work.tile([P, GROUP_J], F32)
             nc.vector.scalar_tensor_tensor(
@@ -275,63 +220,46 @@ def tile_capsulenetwork_pb_kernel(tc, p, Wr, out):
             )
             factors[group] = factor
 
-        def output_bank(group, k):
-            tile_in_group = k // 2
-            half = k % 2
-            t = GROUP_TILES * (group % GROUPS_PER_CHUNK) + tile_in_group
+        def stage_output(group):
             c = group // GROUPS_PER_CHUNK
-            first_col = c * CHUNK + half * BANK
-            acc = psum_out.tile([P, HIGH_PER_BANK, J_CHUNK, O_LOW], F32)
-            nc.tensor.matmul_mx(
-                out=acc[:].rearrange("r h j l -> r (h j l)"),
-                lhsT=p_codes[:, t * P : (t + 1) * P].bitcast(FP8X4),
-                lhsT_scale=p_scales[:, t * P : (t + 1) * P],
-                rhs=w_codes[:, first_col : first_col + BANK].bitcast(FP8X4),
-                rhs_scale=w_scales[:, first_col : first_col + BANK],
-                start=True,
-                stop=True,
-            )
-            if half == 0:
-                result_tile = results.tile([P, J_CHUNK, O_HIGH, O_LOW], F32)
-                result[group] = result_tile
-            nc.vector.tensor_tensor(
-                out=result[group][:, :, half * HIGH_PER_BANK : (half + 1) * HIGH_PER_BANK, :],
-                in0=acc[:].rearrange("r h j l -> r j h l"),
-                in1=factors[group][:, tile_in_group * J_CHUNK : (tile_in_group + 1) * J_CHUNK]
-                .unsqueeze(2)
-                .unsqueeze(3)
-                .to_broadcast([P, J_CHUNK, HIGH_PER_BANK, O_LOW]),
-                op=ALU.mult,
-            )
-            if half == 1:
+            for tile_in_group in range(GROUP_TILES):
+                t = GROUP_TILES * (group % GROUPS_PER_CHUNK) + tile_in_group
+                result = results.tile([P, J_CHUNK, O], F32)
+                for bank in range(CHUNK // BANK):
+                    first_col = c * CHUNK + bank * BANK
+                    acc = psum_out.tile([P, O_PER_BANK, J_CHUNK], F32)
+                    nc.tensor.matmul_mx(
+                        out=acc[:].rearrange("r o j -> r (o j)"),
+                        lhsT=p_codes[:, t * P : (t + 1) * P].bitcast(FP8X4),
+                        lhsT_scale=p_scales[:, t * P : (t + 1) * P],
+                        rhs=w_codes[:, first_col : first_col + BANK].bitcast(FP8X4),
+                        rhs_scale=w_scales[:, first_col : first_col + BANK],
+                        start=True,
+                        stop=True,
+                    )
+                    nc.vector.tensor_tensor(
+                        out=result[:, :, bank * O_PER_BANK : (bank + 1) * O_PER_BANK],
+                        in0=acc[:].rearrange("r o j -> r j o"),
+                        in1=factors[group][:, tile_in_group * J_CHUNK : (tile_in_group + 1) * J_CHUNK]
+                        .unsqueeze(2)
+                        .to_broadcast([P, J_CHUNK, O_PER_BANK]),
+                        op=ALU.mult,
+                    )
                 nc.sync.dma_start(
                     out=out_rows[:, t, c * CHUNK : (c + 1) * CHUNK],
-                    in_=result[group][:].rearrange("r j h l -> r (j h l)"),
+                    in_=result[:].rearrange("r j o -> r (j o)"),
                 )
 
+        prepare_w(0)
+        prepare_p()
         for i in range(N_GROUPS + LAG_OUTPUT):
-            prepare = 1 <= i < N_CHUNKS
-            if prepare:
-                sort_w(i)
-            for k in range(GROUP_BANKS):
-                if i < N_GROUPS:
-                    square_bank(i, k)
-                if k == 0 and i >= LAG_OUTPUT:
-                    factor_newton(i - LAG_OUTPUT)
-                if 0 <= i - LAG_FACTOR < N_GROUPS:
-                    if k == 0:
-                        factor_lengths(i - LAG_FACTOR)
-                    if k == 1:
-                        factor_one_plus_q(i - LAG_FACTOR)
-                    if k == 2:
-                        factor_denominator(i - LAG_FACTOR)
-                    if k == 3:
-                        factor_seed(i - LAG_FACTOR)
-                if i >= LAG_OUTPUT:
-                    output_bank(i - LAG_OUTPUT, k)
-                if prepare:
-                    turn_w(i, k, on_vector=(i < LAG_OUTPUT))
-            if prepare:
-                quantise_w(i)
+            if 1 <= i < N_CHUNKS:
+                prepare_w(i)
+            if i < N_GROUPS:
+                stage_squares(i)
+            if 0 <= i - LAG_FACTOR < N_GROUPS:
+                stage_factor(i - LAG_FACTOR)
+            if 0 <= i - LAG_OUTPUT:
+                stage_output(i - LAG_OUTPUT)
             if 0 <= i - LAG_SUMS < N_GROUPS:
-                sum_squares(i - LAG_SUMS)
+                stage_sums(i - LAG_SUMS)

@@ -27,9 +27,11 @@ QUARTERS = BANK // P
 J_CHUNK = 64
 CHUNK = J_CHUNK * O
 N_CHUNKS = J // J_CHUNK
-O_PER_OPERAND = P // J_CHUNK
-O_PAIRS = O // O_PER_OPERAND
-O_PER_BANK = BANK // J_CHUNK
+O_LOW = 4
+O_HIGH = O // O_LOW
+OPERANDS = CHUNK // P
+OPERANDS_PER_HIGH = OPERANDS // O_HIGH
+HIGH_PER_BANK = BANK // (J_CHUNK * O_LOW)
 
 GROUP_TILES = 2
 GROUP_ROWS = GROUP_TILES * P
@@ -105,14 +107,18 @@ def tile_capsulenetwork_pb_kernel(tc, p, Wr, out):
             )
             w_words = w_sorted[:].bitcast(F32)
             w_grouped = wprep.tile([P, CHUNK * PACK], BF16, align_bytes=64)
-            for bank in range(O // QUARTERS):
+            for oh in range(O_HIGH):
                 turned = psum_brief.tile([P, BANK], F32, tag="brief")
-                for quarter in range(QUARTERS):
-                    o = QUARTERS * bank + quarter
-                    nc.tensor.transpose(
-                        turned[:, quarter * P : (quarter + 1) * P], w_words[:, o * P : (o + 1) * P], ident[:]
-                    )
-                copy_out_of_psum(bank, w_grouped[:].bitcast(F32)[:, bank * BANK : (bank + 1) * BANK], turned[:])
+                for ol in range(O_LOW):
+                    o = O_LOW * oh + ol
+                    nc.tensor.transpose(turned[:, ol * P : (ol + 1) * P], w_words[:, o * P : (o + 1) * P], ident[:])
+                copy_out_of_psum(
+                    oh,
+                    w_grouped[:].bitcast(F32)[:, oh * BANK : (oh + 1) * BANK].rearrange(
+                        "m (j l u) -> m j l u", l=O_LOW, u=HALVES
+                    ),
+                    turned[:].rearrange("m (l j u) -> m j l u", l=O_LOW, u=HALVES),
+                )
             chunk_cols = slice(c * CHUNK, (c + 1) * CHUNK)
             nc.vector.quantize_mx(
                 out=w_codes[:, chunk_cols].bitcast(FP8X4), scales=w_scales[:, chunk_cols], in_=w_grouped[:]
@@ -147,13 +153,13 @@ def tile_capsulenetwork_pb_kernel(tc, p, Wr, out):
                 )
 
         squares = {}
-        pair_sums = {}
+        partial_sums = {}
         factors = {}
 
         def stage_squares(group):
             first_row = (group % GROUPS_PER_CHUNK) * GROUP_ROWS
-            squares_tile = work.tile([P, O_PAIRS, GROUP_ROWS], F32)
-            for bank in range(O_PAIRS // OPERANDS_PER_BANK):
+            squares_tile = work.tile([P, OPERANDS, GROUP_ROWS], F32)
+            for bank in range(OPERANDS // OPERANDS_PER_BANK):
                 acc = psum_brief.tile([P, OPERANDS_PER_BANK, GROUP_ROWS], F32, tag="brief")
                 for operand in range(OPERANDS_PER_BANK):
                     first_col = (group // GROUPS_PER_CHUNK) * CHUNK + (bank * OPERANDS_PER_BANK + operand) * P
@@ -175,24 +181,27 @@ def tile_capsulenetwork_pb_kernel(tc, p, Wr, out):
             squares[group] = squares_tile
 
         def stage_sums(group):
-            sums = psum_sums.tile([P, GROUP_TILES, P], F32)
+            sums = psum_sums.tile([P, GROUP_TILES, OPERANDS_PER_HIGH, P], F32)
             for tile_in_group in range(GROUP_TILES):
-                for o_pair in range(O_PAIRS):
-                    nc.tensor.matmul(
-                        out=sums[:, tile_in_group, :],
-                        lhsT=squares[group][:, o_pair, tile_in_group * P : (tile_in_group + 1) * P],
-                        rhs=ident[:],
-                        is_transpose=True,
-                        start=(o_pair == 0),
-                        stop=(o_pair == O_PAIRS - 1),
-                    )
-            pair_sums[group] = sums
+                for operand in range(OPERANDS_PER_HIGH):
+                    for oh in range(O_HIGH):
+                        nc.tensor.matmul(
+                            out=sums[:, tile_in_group, operand, :],
+                            lhsT=squares[group][
+                                :, oh * OPERANDS_PER_HIGH + operand, tile_in_group * P : (tile_in_group + 1) * P
+                            ],
+                            rhs=ident[:],
+                            is_transpose=True,
+                            start=(oh == 0),
+                            stop=(oh == O_HIGH - 1),
+                        )
+            partial_sums[group] = sums
 
         def stage_factor(group):
             q = work.tile([P, GROUP_J], F32)
             nc.vector.tensor_reduce(
-                out=q[:].rearrange("r (t j) -> r t j", t=GROUP_TILES),
-                in_=pair_sums[group][:].rearrange("r t (o j) -> r t j o", o=O_PER_OPERAND),
+                out=q[:],
+                in_=partial_sums[group][:].rearrange("r t b (j l) -> r (t b j) l", l=O_LOW),
                 axis=mybir.AxisListType.X,
                 op=ALU.add,
             )
@@ -224,12 +233,12 @@ def tile_capsulenetwork_pb_kernel(tc, p, Wr, out):
             c = group // GROUPS_PER_CHUNK
             for tile_in_group in range(GROUP_TILES):
                 t = GROUP_TILES * (group % GROUPS_PER_CHUNK) + tile_in_group
-                result = results.tile([P, J_CHUNK, O], F32)
+                result = results.tile([P, J_CHUNK, O_HIGH, O_LOW], F32)
                 for bank in range(CHUNK // BANK):
                     first_col = c * CHUNK + bank * BANK
-                    acc = psum_out.tile([P, O_PER_BANK, J_CHUNK], F32)
+                    acc = psum_out.tile([P, HIGH_PER_BANK, J_CHUNK, O_LOW], F32)
                     nc.tensor.matmul_mx(
-                        out=acc[:].rearrange("r o j -> r (o j)"),
+                        out=acc[:].rearrange("r h j l -> r (h j l)"),
                         lhsT=p_codes[:, t * P : (t + 1) * P].bitcast(FP8X4),
                         lhsT_scale=p_scales[:, t * P : (t + 1) * P],
                         rhs=w_codes[:, first_col : first_col + BANK].bitcast(FP8X4),
@@ -238,16 +247,17 @@ def tile_capsulenetwork_pb_kernel(tc, p, Wr, out):
                         stop=True,
                     )
                     nc.vector.tensor_tensor(
-                        out=result[:, :, bank * O_PER_BANK : (bank + 1) * O_PER_BANK],
-                        in0=acc[:].rearrange("r o j -> r j o"),
+                        out=result[:, :, bank * HIGH_PER_BANK : (bank + 1) * HIGH_PER_BANK, :],
+                        in0=acc[:].rearrange("r h j l -> r j h l"),
                         in1=factors[group][:, tile_in_group * J_CHUNK : (tile_in_group + 1) * J_CHUNK]
                         .unsqueeze(2)
-                        .to_broadcast([P, J_CHUNK, O_PER_BANK]),
+                        .unsqueeze(3)
+                        .to_broadcast([P, J_CHUNK, HIGH_PER_BANK, O_LOW]),
                         op=ALU.mult,
                     )
                 nc.sync.dma_start(
                     out=out_rows[:, t, c * CHUNK : (c + 1) * CHUNK],
-                    in_=result[:].rearrange("r j o -> r (j o)"),
+                    in_=result[:].rearrange("r j h l -> r (j h l)"),
                 )
 
         prepare_w(0)

from contextlib import ExitStack

import concourse.mybir as mybir
from concourse.masks import make_identity

F32 = mybir.dt.float32
BF16 = mybir.dt.bfloat16
U32 = mybir.dt.uint32
U8 = mybir.dt.uint8
FP8X4 = mybir.dt.float8_e4m3fn_x4
ACT = mybir.ActivationFunctionType
ALU = mybir.AluOpType

P = 128
PACK = 4
HALVES = 2
B = 1024
K = 512
I = 16
J = 256
O = 16
COLS = J * O
B_TILES = B // P
N_HALF = K // I // HALVES
BANK = 512
QUARTERS = BANK // P
J_CHUNK = 64
CHUNK = J_CHUNK * O
N_CHUNKS = J // J_CHUNK
O_LOW = 4
O_HIGH = O // O_LOW
OPERANDS = CHUNK // P
OPERANDS_PER_HIGH = OPERANDS // O_HIGH
HIGH_PER_BANK = BANK // (J_CHUNK * O_LOW)

GROUP_TILES = 2
GROUP_ROWS = GROUP_TILES * P
GROUP_J = GROUP_TILES * J_CHUNK
GROUPS_PER_CHUNK = B_TILES // GROUP_TILES
N_GROUPS = N_CHUNKS * GROUPS_PER_CHUNK
OPERANDS_PER_BANK = BANK // GROUP_ROWS
LAG_SUMS = 1
LAG_FACTOR = 2
LAG_OUTPUT = 3

COUPLING = 1.0 / 256.0
SQ_EPS = 1e-8
SHRINK = 2.0 ** -32

FLOPS = 2 * B * K * COLS


def tile_capsulenetwork_pb_kernel(tc, p, Wr, out):
    nc = tc.nc
    out_rows = out.rearrange("(r t) j o -> r t (j o)", t=B_TILES)

    with ExitStack() as ctx:
        keep = ctx.enter_context(tc.tile_pool(name="keep", bufs=1))
        wload = ctx.enter_context(tc.tile_pool(name="wload", bufs=N_CHUNKS))
        wprep = ctx.enter_context(tc.tile_pool(name="wprep", bufs=2))
        work = ctx.enter_context(tc.tile_pool(name="work", bufs=3))
        results = ctx.enter_context(tc.tile_pool(name="results", bufs=2 * GROUP_TILES))
        psum_brief = ctx.enter_context(tc.psum_pool(name="psum_brief", bufs=3))
        psum_sums = ctx.enter_context(tc.psum_pool(name="psum_sums", bufs=2))
        psum_out = ctx.enter_context(tc.psum_pool(name="psum_out", bufs=3))

        def load_w_chunk(c):
            w_raw = wload.tile([P, N_HALF, O * I], BF16)
            for u in range(HALVES):
                nc.sync.dma_start(
                    out=w_raw[u:P:HALVES, :, :],
                    in_=Wr[
                        u * N_HALF : (u + 1) * N_HALF, c * J_CHUNK : (c + 1) * J_CHUNK, :, :
                    ].rearrange("n j o i -> j n (o i)"),
                )
            return w_raw

        w_raws = [load_w_chunk(0)]
        p_raw = keep.tile([P, B_TILES * K], BF16)
        nc.sync.dma_start(out=p_raw[:], in_=p.rearrange("(r t) n i -> r (t n i)", t=B_TILES))
        w_raws.extend([load_w_chunk(c) for c in range(1, N_CHUNKS)])

        shrink_col = keep.tile([P, 1], F32)
        nc.vector.memset(shrink_col[:], SHRINK)
        table_warmer = keep.tile([P, 1], F32)
        nc.scalar.activation(out=table_warmer[:], in_=shrink_col[:], func=ACT.Abs_reciprocal_sqrt)

        ident = keep.tile([P, P], F32)
        make_identity(nc, ident[:])

        p_codes = keep.tile([P, B_TILES * P], U32, align_bytes=64)
        p_scales = keep.tile([P, B_TILES * P], U8, align_bytes=64)
        w_codes = keep.tile([P, COLS], U32, align_bytes=64)
        w_scales = keep.tile([P, COLS], U8, align_bytes=64)

        def copy_out_of_psum(bank, out_view, in_view):
            if bank % 2 == 0:
                nc.scalar.copy(out=out_view, in_=in_view)
            else:
                nc.vector.tensor_copy(out=out_view, in_=in_view)

        def prepare_w(c):
            w_sorted = wprep.tile([P, O * N_HALF * I], BF16)
            nc.vector.tensor_copy(
                out=w_sorted[:].rearrange("q (o n i) -> q o n i", o=O, i=I),
                in_=w_raws[c][:].rearrange("q n (o i) -> q o n i", i=I),
            )
            w_words = w_sorted[:].bitcast(F32)
            w_grouped = wprep.tile([P, CHUNK * PACK], BF16, align_bytes=64)
            for oh in range(O_HIGH):
                turned = psum_brief.tile([P, BANK], F32, tag="brief")
                for ol in range(O_LOW):
                    o = O_LOW * oh + ol
                    nc.tensor.transpose(turned[:, ol * P : (ol + 1) * P], w_words[:, o * P : (o + 1) * P], ident[:])
                copy_out_of_psum(
                    oh,
                    w_grouped[:].bitcast(F32)[:, oh * BANK : (oh + 1) * BANK].rearrange(
                        "m (j l u) -> m j l u", l=O_LOW, u=HALVES
                    ),
                    turned[:].rearrange("m (l j u) -> m j l u", l=O_LOW, u=HALVES),
                )
            chunk_cols = slice(c * CHUNK, (c + 1) * CHUNK)
            nc.vector.quantize_mx(
                out=w_codes[:, chunk_cols].bitcast(FP8X4), scales=w_scales[:, chunk_cols], in_=w_grouped[:]
            )

        def prepare_p():
            p_words = p_raw[:].bitcast(F32)
            p_grouped = keep.tile([P, B_TILES * P * PACK], BF16, align_bytes=64)
            p_grouped_words = p_grouped[:].bitcast(F32)
            for bank in range(GROUPS_PER_CHUNK):
                turned = psum_brief.tile([P, BANK], F32, tag="brief")
                for quarter in range(QUARTERS):
                    first_word = (bank * QUARTERS + quarter) * P
                    nc.tensor.transpose(
                        turned[:, quarter * P : (quarter + 1) * P],
                        p_words[:, first_word : first_word + P],
                        ident[:],
                    )
                copy_out_of_psum(
                    bank,
                    p_grouped_words[:, bank * BANK : (bank + 1) * BANK].rearrange(
                        "m (t r u) -> m t r u", t=GROUP_TILES, u=HALVES
                    ),
                    turned[:].rearrange("m (t u r) -> m t r u", t=GROUP_TILES, u=HALVES),
                )
            for bank in range(GROUPS_PER_CHUNK):
                rows = slice(bank * GROUP_ROWS, (bank + 1) * GROUP_ROWS)
                nc.vector.quantize_mx(
                    out=p_codes[:, rows].bitcast(FP8X4),
                    scales=p_scales[:, rows],
                    in_=p_grouped[:, bank * GROUP_ROWS * PACK : (bank + 1) * GROUP_ROWS * PACK],
                )

        squares = {}
        partial_sums = {}
        factors = {}

        def stage_squares(group):
            first_row = (group % GROUPS_PER_CHUNK) * GROUP_ROWS
            squares_tile = work.tile([P, OPERANDS, GROUP_ROWS], F32)
            for bank in range(OPERANDS // OPERANDS_PER_BANK):
                acc = psum_brief.tile([P, OPERANDS_PER_BANK, GROUP_ROWS], F32, tag="brief")
                for operand in range(OPERANDS_PER_BANK):
                    first_col = (group // GROUPS_PER_CHUNK) * CHUNK + (bank * OPERANDS_PER_BANK + operand) * P
                    nc.tensor.matmul_mx(
                        out=acc[:, operand, :],
                        lhsT=w_codes[:, first_col : first_col + P].bitcast(FP8X4),
                        lhsT_scale=w_scales[:, first_col : first_col + P],
                        rhs=p_codes[:, first_row : first_row + GROUP_ROWS].bitcast(FP8X4),
                        rhs_scale=p_scales[:, first_row : first_row + GROUP_ROWS],
                        start=True,
                        stop=True,
                    )
                nc.scalar.activation(
                    out=squares_tile[:, bank * OPERANDS_PER_BANK : (bank + 1) * OPERANDS_PER_BANK, :],
                    in_=acc[:],
                    func=ACT.Square,
                    scale=COUPLING,
                )
            squares[group] = squares_tile

        def stage_sums(group):
            sums = psum_sums.tile([P, GROUP_TILES, OPERANDS_PER_HIGH, P], F32)
            for tile_in_group in range(GROUP_TILES):
                for operand in range(OPERANDS_PER_HIGH):
                    for oh in range(O_HIGH):
                        nc.tensor.matmul(
                            out=sums[:, tile_in_group, operand, :],
                            lhsT=squares[group][
                                :, oh * OPERANDS_PER_HIGH + operand, tile_in_group * P : (tile_in_group + 1) * P
                            ],
                            rhs=ident[:],
                            is_transpose=True,
                            start=(oh == 0),
                            stop=(oh == O_HIGH - 1),
                        )
            partial_sums[group] = sums

        def stage_factor(group):
            q = work.tile([P, GROUP_J], F32)
            nc.vector.tensor_reduce(
                out=q[:],
                in_=partial_sums[group][:].rearrange("r t b (j l) -> r (t b j) l", l=O_LOW),
                axis=mybir.AxisListType.X,
                op=ALU.add,
            )
            one_plus_q_sq = work.tile([P, GROUP_J], F32)
            nc.scalar.activation(
                out=one_plus_q_sq[:], in_=q[:], func=ACT.Square, scale=SHRINK, bias=shrink_col[:]
            )
            x = work.tile([P, GROUP_J], F32)
            nc.vector.scalar_tensor_tensor(
                out=x[:], in0=q[:], scalar=SQ_EPS, in1=one_plus_q_sq[:], op0=ALU.add, op1=ALU.mult
            )
            y = work.tile([P, GROUP_J], F32)
            nc.scalar.activation(out=y[:], in_=x[:], func=ACT.Abs_reciprocal_sqrt)
            y_sq = work.tile([P, GROUP_J], F32)
            nc.scalar.activation(out=y_sq[:], in_=y[:], func=ACT.Square)
            x_y_sq = work.tile([P, GROUP_J], F32)
            nc.vector.tensor_tensor(out=x_y_sq[:], in0=x[:], in1=y_sq[:], op=ALU.mult)
            rough = work.tile([P, GROUP_J], F32)
            nc.vector.scalar_tensor_tensor(
                out=rough[:], in0=q[:], scalar=-0.5 * SHRINK * COUPLING, in1=y[:], op0=ALU.mult, op1=ALU.mult
            )
            factor = work.tile([P, GROUP_J], F32)
            nc.vector.scalar_tensor_tensor(
                out=factor[:], in0=x_y_sq[:], scalar=3.0, in1=rough[:], op0=ALU.subtract, op1=ALU.mult
            )
            factors[group] = factor

        def stage_output(group):
            c = group // GROUPS_PER_CHUNK
            for tile_in_group in range(GROUP_TILES):
                t = GROUP_TILES * (group % GROUPS_PER_CHUNK) + tile_in_group
                result = results.tile([P, J_CHUNK, O_HIGH, O_LOW], F32)
                for bank in range(CHUNK // BANK):
                    first_col = c * CHUNK + bank * BANK
                    acc = psum_out.tile([P, HIGH_PER_BANK, J_CHUNK, O_LOW], F32)
                    nc.tensor.matmul_mx(
                        out=acc[:].rearrange("r h j l -> r (h j l)"),
                        lhsT=p_codes[:, t * P : (t + 1) * P].bitcast(FP8X4),
                        lhsT_scale=p_scales[:, t * P : (t + 1) * P],
                        rhs=w_codes[:, first_col : first_col + BANK].bitcast(FP8X4),
                        rhs_scale=w_scales[:, first_col : first_col + BANK],
                        start=True,
                        stop=True,
                    )
                    nc.vector.tensor_tensor(
                        out=result[:, :, bank * HIGH_PER_BANK : (bank + 1) * HIGH_PER_BANK, :],
                        in0=acc[:].rearrange("r h j l -> r j h l"),
                        in1=factors[group][:, tile_in_group * J_CHUNK : (tile_in_group + 1) * J_CHUNK]
                        .unsqueeze(2)
                        .unsqueeze(3)
                        .to_broadcast([P, J_CHUNK, HIGH_PER_BANK, O_LOW]),
                        op=ALU.mult,
                    )
                nc.sync.dma_start(
                    out=out_rows[:, t, c * CHUNK : (c + 1) * CHUNK],
                    in_=result[:].rearrange("r j h l -> r (j h l)"),
                )

        prepare_w(0)
        prepare_p()
        for i in range(N_GROUPS + LAG_OUTPUT):
            if 1 <= i < N_CHUNKS:
                prepare_w(i)
            if i < N_GROUPS:
                stage_squares(i)
            if 0 <= i - LAG_FACTOR < N_GROUPS:
                stage_factor(i - LAG_FACTOR)
            if 0 <= i - LAG_OUTPUT:
                stage_output(i - LAG_OUTPUT)
            if 0 <= i - LAG_SUMS < N_GROUPS:
                stage_sums(i - LAG_SUMS)
